import numpy as np
import ml_dtypes


def mxq(x, axis, fmt="e4m3"):
    dtype, down = {"e4m3": (ml_dtypes.float8_e4m3fn, 7), "e5m2": (ml_dtypes.float8_e5m2, 14)}[fmt]
    v = np.moveaxis(np.asarray(x, np.float32).astype(ml_dtypes.bfloat16).astype(np.float64), axis, -1)
    blocks = v.reshape(v.shape[:-1] + (-1, 32))
    amax = np.abs(blocks).max(-1, keepdims=True)
    byte = np.maximum(np.where(amax > 0, np.frexp(amax)[1] - 1 + 127, 0) - down, 1)
    scale = np.exp2(byte - 127.0)
    codes = (blocks / scale).astype(np.float32).astype(dtype).astype(np.float64)
    return np.moveaxis((codes * scale).reshape(v.shape), -1, axis)


WIDE = False


def mx_kscale(k):
    if not WIDE:
        return np.ones(k)
    levels = np.array([10, -10, 5, -5, 0])
    a = np.random.permutation(np.resize(levels, k // 512 * 4)).reshape(k // 512, 4)
    idx = np.arange(k)
    return np.exp2(a[idx // 512, idx % 128 // 32])


BF16 = ml_dtypes.bfloat16


def bf(x):
    return np.asarray(x, np.float32).astype(BF16)


def f64(x):
    return np.asarray(x).astype(np.float64)


E2M1 = np.array([0.0, 0.5, 1.0, 1.5, 2.0, 3.0, 4.0, 6.0, -0.0, -0.5, -1.0, -1.5, -2.0, -3.0, -4.0, -6.0])


def pack_weight(w, fmt):
    k, n = w.shape
    w = f64(bf(w)).reshape(k // 32, 32, n)
    amax = np.abs(w).max(1)
    if fmt == "e4m3":
        byte = np.frexp(amax)[1] - 1 + 127 - 7
    else:
        mant, ex = np.frexp(amax / 6.0)
        byte = np.where(mant > 0.5, ex, ex - 1) + 127
    byte = np.clip(np.where(amax > 0, byte, 1), 1, 254)
    scaled = (w * np.exp2(127.0 - byte)[:, None, :]).reshape(k, n).astype(np.float32)
    by_word = np.ascontiguousarray(scaled.reshape(k // 512, 128, 4, n).transpose(0, 1, 3, 2))
    if fmt == "e4m3":
        words = by_word.astype(ml_dtypes.float8_e4m3fn).view(np.uint8)
    else:
        c = by_word.astype(ml_dtypes.float4_e2m1fn).view(np.uint8) & 0xF
        words = c[..., 0::2] | (c[..., 1::2] << 4)
    return np.ascontiguousarray(words), np.ascontiguousarray(byte.astype(np.uint8).reshape(k // 512, 16, n))


def unpack_weight(words, scales, fmt):
    g, p, n, _ = words.shape
    if fmt == "e4m3":
        vals = np.ascontiguousarray(words).view(ml_dtypes.float8_e4m3fn).astype(np.float64)
    else:
        nib = np.empty((g, p, n, 4), np.uint8)
        nib[..., 0::2] = words & 0xF
        nib[..., 1::2] = words >> 4
        vals = E2M1[nib]
    vals = vals * np.repeat(np.exp2(scales.astype(np.float64) - 127.0), 8, axis=1)[..., None]
    return vals.transpose(0, 1, 3, 2).reshape(g * 512, n)


B, S, C, H = 1, 1536, 1024, 4096
WS = 1.25
FMT = "e4m3"


def setup_inputs():
    s = mx_kscale(C)
    x = bf(np.random.standard_normal((B, S, C)) * s)
    w = np.random.standard_normal((2 * C, C)) * WS / np.sqrt(C) / s[None, :]
    words, scales = pack_weight(np.ascontiguousarray(w.T), FMT)
    return {"x": x, "w_qk_words": words, "w_qk_scales": scales}


def reference(x, w_qk_words, w_qk_scales):
    qk = unpack_weight(w_qk_words, w_qk_scales, FMT).T @ mxq(f64(x), 2, "e4m3").transpose(0, 2, 1)
    q, k = qk[:, :C, :], qk[:, C:, :]
    return (mxq(q, 2, "e4m3") @ mxq(k, 2, "e4m3").transpose(0, 2, 1)) / np.sqrt(S)

@@ -1,0 +1,180 @@
+import math
+from contextlib import ExitStack
+
+import concourse.mybir as mybir
+from concourse.masks import make_identity
+
+F32 = mybir.dt.float32
+BF16 = mybir.dt.bfloat16
+I32 = mybir.dt.int32
+U32 = mybir.dt.uint32
+U8 = mybir.dt.uint8
+FP8X4 = mybir.dt.float8_e4m3fn_x4
+
+P = 128
+PACK = 4
+K_PASS = P * PACK
+BANK = 512
+PSUM_BANKS = 8
+
+SEQ = 1536
+CH = 1024
+QK = 2 * CH
+
+CH_PASSES = CH // K_PASS
+SEQ_GROUPS = SEQ // K_PASS
+CHUNK = 512
+CHUNKS = QK // CHUNK
+BANKS_PER_CHUNK = CHUNK // P
+
+FLOPS = 2 * QK * SEQ * CH + 2 * CH * CH * SEQ
+
+
+def tile_transformer_block_pa_kernel(tc, x, w_qk_words, w_qk_scales, out):
+    nc = tc.nc
+    with ExitStack() as ctx:
+        keep = ctx.enter_context(tc.tile_pool(name="keep", bufs=1))
+        x_stage = ctx.enter_context(tc.tile_pool(name="x_stage", bufs=4))
+        qk_stage = ctx.enter_context(tc.tile_pool(name="qk_stage", bufs=3))
+        out_stage = ctx.enter_context(tc.tile_pool(name="out_stage", bufs=4))
+        psum = ctx.enter_context(tc.psum_pool(name="psum", bufs=PSUM_BANKS))
+        ctx.enter_context(tc.manual_schedule())
+
+        identity = keep.tile([P, P], F32)
+        x_rows = keep.tile([P, SEQ_GROUPS, PACK, CH], BF16)
+        x_codes = keep.tile([P, SEQ_GROUPS, PACK, CH_PASSES * P], U32, align_bytes=64)
+        x_scales = keep.tile([P, SEQ_GROUPS, PACK, CH_PASSES * P], U8, align_bytes=64)
+        w_codes = keep.tile([P, CH_PASSES, QK], U32, align_bytes=64)
+        w_scales = keep.tile([P, QK], U8, align_bytes=64)
+        qk_codes = keep.tile([P, SEQ_GROUPS, QK], U32, align_bytes=64)
+        qk_scales = keep.tile([P, SEQ_GROUPS, QK], U8, align_bytes=64)
+
+        nc.vector.memset(w_scales[:].bitcast(I32), 0)
+        make_identity(nc, identity[:])
+
+        x_by_lane = x[0].rearrange("(group p lane) c -> group p lane c", p=P, lane=PACK)
+        w_bytes = w_qk_words.rearrange("cpass p n v -> p cpass (n v)")
+
+        def load_x(group):
+            for lane in range(PACK):
+                nc.sync.dma_start(out=x_rows[:, group, lane, :], in_=x_by_lane[group, :, lane, :])
+
+        def load_w_scales():
+            for quarter in range(4):
+                nc.sync.dma_start(
+                    out=w_scales[32 * quarter : 32 * quarter + 4 * CH_PASSES, :].bitcast(I32),
+                    in_=w_qk_scales[:, 4 * quarter : 4 * quarter + 4, :].bitcast(I32),
+                )
+
+        def load_w_codes(chunk):
+            nc.sync.dma_start(
+                out=w_codes[:, :, chunk * CHUNK : (chunk + 1) * CHUNK].bitcast(I32),
+                in_=w_bytes[:, :, chunk * CHUNK * PACK : (chunk + 1) * CHUNK * PACK].bitcast(I32),
+            )
+
+        load_x(0)
+        load_w_scales()
+        load_w_codes(0)
+        load_w_codes(1)
+        load_x(1)
+        load_w_codes(2)
+        load_w_codes(3)
+        load_x(2)
+
+        def copy_out_of_bank(bank_in_four, out_ap, in_ap):
+            if bank_in_four == 0:
+                nc.vector.tensor_copy(out=out_ap, in_=in_ap)
+            else:
+                nc.scalar.copy(out=out_ap, in_=in_ap)
+
+        def transpose_and_quantise_x(group):
+            for lane in range(PACK):
+                pairs = x_rows[:, group, lane, :].bitcast(F32)
+                pairs_t = psum.tile([P, CH_PASSES, 2, P], F32, tag="bank")
+                for cpass in range(CH_PASSES):
+                    for half in range(2):
+                        first = cpass * (K_PASS // 2) + half
+                        nc.tensor.transpose(
+                            pairs_t[:, cpass, half, :],
+                            pairs[:, first : (cpass + 1) * (K_PASS // 2) : 2],
+                            identity[:],
+                        )
+                x_grouped = x_stage.tile([P, CH_PASSES, P, PACK], BF16, align_bytes=64)
+                copy_out_of_bank(
+                    lane,
+                    x_grouped[:].bitcast(F32),
+                    pairs_t[:].rearrange("p cpass half s -> p cpass s half"),
+                )
+                nc.vector.quantize_mx(
+                    out=x_codes[:, group, lane, :].bitcast(FP8X4),
+                    scales=x_scales[:, group, lane, :],
+                    in_=x_grouped[:].rearrange("p cpass s v -> p (cpass s v)"),
+                )
+
+        def project(group, chunk):
+            qk_grouped = qk_stage.tile([P, CHUNK, PACK], BF16, align_bytes=64)
+            for b in range(BANKS_PER_CHUNK):
+                channels = slice(chunk * CHUNK + b * P, chunk * CHUNK + (b + 1) * P)
+                lanes = psum.tile([P, PACK, P], F32, tag="bank")
+                for lane in range(PACK):
+                    for cpass in range(CH_PASSES):
+                        positions = slice(cpass * P, (cpass + 1) * P)
+                        nc.tensor.matmul_mx(
+                            out=lanes[:, lane, :],
+                            lhsT=x_codes[:, group, lane, positions].bitcast(FP8X4),
+                            lhsT_scale=x_scales[:, group, lane, positions],
+                            rhs=w_codes[:, cpass, channels].bitcast(FP8X4),
+                            rhs_scale=w_scales[4 * cpass : P, channels],
+                            start=(cpass == 0),
+                            stop=(cpass == CH_PASSES - 1),
+                        )
+                copy_out_of_bank(
+                    b,
+                    qk_grouped[:, b * P : (b + 1) * P, :],
+                    lanes[:].rearrange("p lane n -> p n lane"),
+                )
+            return qk_grouped
+
+        def quantise_qk(qk_grouped, group, chunk):
+            channels = slice(chunk * CHUNK, (chunk + 1) * CHUNK)
+            nc.vector.quantize_mx(
+                out=qk_codes[:, group, channels].bitcast(FP8X4),
+                scales=qk_scales[:, group, channels],
+                in_=qk_grouped[:].rearrange("p n lane -> p (n lane)"),
+            )
+
+        transpose_and_quantise_x(0)
+        not_yet_quantised = None
+        for group in range(SEQ_GROUPS):
+            for chunk in range(CHUNKS):
+                qk_grouped = project(group, chunk)
+                if not_yet_quantised is not None:
+                    quantise_qk(*not_yet_quantised)
+                not_yet_quantised = (qk_grouped, group, chunk)
+                if chunk == CHUNKS // 2 - 1 and group + 1 < SEQ_GROUPS:
+                    transpose_and_quantise_x(group + 1)
+        quantise_qk(*not_yet_quantised)
+
+        for k_half in range(CH // BANK):
+            k_channels = slice(CH + k_half * BANK, CH + (k_half + 1) * BANK)
+            for q_tile in range(CH // P):
+                q_channels = slice(q_tile * P, (q_tile + 1) * P)
+                sums = psum.tile([P, BANK], F32, tag="bank")
+                for group in range(SEQ_GROUPS):
+                    nc.tensor.matmul_mx(
+                        out=sums[:],
+                        lhsT=qk_codes[:, group, q_channels].bitcast(FP8X4),
+                        lhsT_scale=qk_scales[:, group, q_channels],
+                        rhs=qk_codes[:, group, k_channels].bitcast(FP8X4),
+                        rhs_scale=qk_scales[:, group, k_channels],
+                        start=(group == 0),
+                        stop=(group == SEQ_GROUPS - 1),
+                    )
+                score = out_stage.tile([P, BANK], F32)
+                if q_tile % 2 == 0:
+                    nc.scalar.mul(out=score[:], in_=sums[:], mul=1.0 / math.sqrt(SEQ))
+                else:
+                    nc.vector.tensor_scalar_mul(out=score[:], in0=sums[:], scalar1=1.0 / math.sqrt(SEQ))
+                nc.sync.dma_start(
+                    out=out[0, q_channels, k_half * BANK : (k_half + 1) * BANK], in_=score[:]
+                )

@@ -34,6 +34,7 @@ def tile_transformer_block_pa_kernel(tc, x, w_qk_words, w_qk_scales, out):
     nc = tc.nc
     with ExitStack() as ctx:
         keep = ctx.enter_context(tc.tile_pool(name="keep", bufs=1))
+        x_sort = ctx.enter_context(tc.tile_pool(name="x_sort", bufs=2))
         x_stage = ctx.enter_context(tc.tile_pool(name="x_stage", bufs=4))
         qk_stage = ctx.enter_context(tc.tile_pool(name="qk_stage", bufs=3))
         out_stage = ctx.enter_context(tc.tile_pool(name="out_stage", bufs=4))
@@ -88,16 +89,20 @@ def tile_transformer_block_pa_kernel(tc, x, w_qk_words, w_qk_scales, out):
                 nc.scalar.copy(out=out_ap, in_=in_ap)
 
         def transpose_and_quantise_x(group):
+            pairs = x_sort.tile([P, PACK, CH_PASSES, 2, P], F32)
             for lane in range(PACK):
-                pairs = x_rows[:, group, lane, :].bitcast(F32)
+                nc.vector.tensor_copy(
+                    out=pairs[:, lane, :, :, :],
+                    in_=x_rows[:, group, lane, :]
+                    .bitcast(F32)
+                    .rearrange("p (cpass k half) -> p cpass half k", cpass=CH_PASSES, half=2),
+                )
+            for lane in range(PACK):
                 pairs_t = psum.tile([P, CH_PASSES, 2, P], F32, tag="bank")
                 for cpass in range(CH_PASSES):
                     for half in range(2):
-                        first = cpass * (K_PASS // 2) + half
                         nc.tensor.transpose(
-                            pairs_t[:, cpass, half, :],
-                            pairs[:, first : (cpass + 1) * (K_PASS // 2) : 2],
-                            identity[:],
+                            pairs_t[:, cpass, half, :], pairs[:, lane, cpass, half, :], identity[:]
                         )
                 x_grouped = x_stage.tile([P, CH_PASSES, P, PACK], BF16, align_bytes=64)
                 copy_out_of_bank(

@@ -88,7 +88,7 @@ def tile_transformer_block_pa_kernel(tc, x, w_qk_words, w_qk_scales, out):
             else:
                 nc.scalar.copy(out=out_ap, in_=in_ap)
 
-        def transpose_and_quantise_x(group):
+        def sort_x(group):
             pairs = x_sort.tile([P, PACK, CH_PASSES, 2, P], F32)
             for lane in range(PACK):
                 nc.vector.tensor_copy(
@@ -97,6 +97,9 @@ def tile_transformer_block_pa_kernel(tc, x, w_qk_words, w_qk_scales, out):
                     .bitcast(F32)
                     .rearrange("p (cpass k half) -> p cpass half k", cpass=CH_PASSES, half=2),
                 )
+            return pairs
+
+        def transpose_and_quantise_x(group, pairs):
             for lane in range(PACK):
                 pairs_t = psum.tile([P, CH_PASSES, 2, P], F32, tag="bank")
                 for cpass in range(CH_PASSES):
@@ -117,15 +120,16 @@ def tile_transformer_block_pa_kernel(tc, x, w_qk_words, w_qk_scales, out):
                 )
 
         def project(group, chunk):
-            qk_grouped = qk_stage.tile([P, CHUNK, PACK], BF16, align_bytes=64)
-            for b in range(BANKS_PER_CHUNK):
-                channels = slice(chunk * CHUNK + b * P, chunk * CHUNK + (b + 1) * P)
-                lanes = psum.tile([P, PACK, P], F32, tag="bank")
-                for lane in range(PACK):
+            banks = [
+                psum.tile([P, PACK, P], F32, tag="bank", name="lanes%d" % b) for b in range(BANKS_PER_CHUNK)
+            ]
+            for lane in range(PACK):
+                for b in range(BANKS_PER_CHUNK):
+                    channels = slice(chunk * CHUNK + b * P, chunk * CHUNK + (b + 1) * P)
                     for cpass in range(CH_PASSES):
                         positions = slice(cpass * P, (cpass + 1) * P)
                         nc.tensor.matmul_mx(
-                            out=lanes[:, lane, :],
+                            out=banks[b][:, lane, :],
                             lhsT=x_codes[:, group, lane, positions].bitcast(FP8X4),
                             lhsT_scale=x_scales[:, group, lane, positions],
                             rhs=w_codes[:, cpass, channels].bitcast(FP8X4),
@@ -133,10 +137,15 @@ def tile_transformer_block_pa_kernel(tc, x, w_qk_words, w_qk_scales, out):
                             start=(cpass == 0),
                             stop=(cpass == CH_PASSES - 1),
                         )
+            return banks
+
+        def round_and_group(banks):
+            qk_grouped = qk_stage.tile([P, CHUNK, PACK], BF16, align_bytes=64)
+            for b in range(BANKS_PER_CHUNK):
                 copy_out_of_bank(
                     b,
                     qk_grouped[:, b * P : (b + 1) * P, :],
-                    lanes[:].rearrange("p lane n -> p n lane"),
+                    banks[b][:].rearrange("p lane n -> p n lane"),
                 )
             return qk_grouped
 
@@ -148,16 +157,18 @@ def tile_transformer_block_pa_kernel(tc, x, w_qk_words, w_qk_scales, out):
                 in_=qk_grouped[:].rearrange("p n lane -> p (n lane)"),
             )
 
-        transpose_and_quantise_x(0)
+        transpose_and_quantise_x(0, sort_x(0))
         not_yet_quantised = None
         for group in range(SEQ_GROUPS):
             for chunk in range(CHUNKS):
-                qk_grouped = project(group, chunk)
+                banks = project(group, chunk)
                 if not_yet_quantised is not None:
                     quantise_qk(*not_yet_quantised)
-                not_yet_quantised = (qk_grouped, group, chunk)
-                if chunk == CHUNKS // 2 - 1 and group + 1 < SEQ_GROUPS:
-                    transpose_and_quantise_x(group + 1)
+                not_yet_quantised = (round_and_group(banks), group, chunk)
+                if chunk == 0 and group + 1 < SEQ_GROUPS:
+                    next_pairs = sort_x(group + 1)
+                if chunk == 1 and group + 1 < SEQ_GROUPS:
+                    transpose_and_quantise_x(group + 1, next_pairs)
         quantise_qk(*not_yet_quantised)
 
         for k_half in range(CH // BANK):

@@ -24,8 +24,8 @@ QK = 2 * CH
 CH_PASSES = CH // K_PASS
 SEQ_GROUPS = SEQ // K_PASS
 CHUNK = 512
-CHUNKS = QK // CHUNK
-BANKS_PER_CHUNK = CHUNK // P
+HALF = CHUNK // 2
+CHUNK_ORDER = (2, 0, 1, 3)
 
 FLOPS = 2 * QK * SEQ * CH + 2 * CH * CH * SEQ
 
@@ -36,8 +36,9 @@ def tile_transformer_block_pa_kernel(tc, x, w_qk_words, w_qk_scales, out):
         keep = ctx.enter_context(tc.tile_pool(name="keep", bufs=1))
         x_sort = ctx.enter_context(tc.tile_pool(name="x_sort", bufs=2))
         x_stage = ctx.enter_context(tc.tile_pool(name="x_stage", bufs=4))
+        qk_pairs = ctx.enter_context(tc.tile_pool(name="qk_pairs", bufs=3))
         qk_stage = ctx.enter_context(tc.tile_pool(name="qk_stage", bufs=3))
-        out_stage = ctx.enter_context(tc.tile_pool(name="out_stage", bufs=4))
+        out_stage = ctx.enter_context(tc.tile_pool(name="out_stage", bufs=16))
         psum = ctx.enter_context(tc.psum_pool(name="psum", bufs=PSUM_BANKS))
         ctx.enter_context(tc.manual_schedule())
 
@@ -75,18 +76,12 @@ def tile_transformer_block_pa_kernel(tc, x, w_qk_words, w_qk_scales, out):
 
         load_x(0)
         load_w_scales()
-        load_w_codes(0)
-        load_w_codes(1)
+        load_w_codes(CHUNK_ORDER[0])
+        load_w_codes(CHUNK_ORDER[1])
         load_x(1)
-        load_w_codes(2)
-        load_w_codes(3)
+        load_w_codes(CHUNK_ORDER[2])
+        load_w_codes(CHUNK_ORDER[3])
         load_x(2)
-
-        def copy_out_of_bank(bank_in_four, out_ap, in_ap):
-            if bank_in_four == 0:
-                nc.vector.tensor_copy(out=out_ap, in_=in_ap)
-            else:
-                nc.scalar.copy(out=out_ap, in_=in_ap)
 
         def sort_x(group):
             pairs = x_sort.tile([P, PACK, CH_PASSES, 2, P], F32)
@@ -108,10 +103,10 @@ def tile_transformer_block_pa_kernel(tc, x, w_qk_words, w_qk_scales, out):
                             pairs_t[:, cpass, half, :], pairs[:, lane, cpass, half, :], identity[:]
                         )
                 x_grouped = x_stage.tile([P, CH_PASSES, P, PACK], BF16, align_bytes=64)
-                copy_out_of_bank(
-                    lane,
-                    x_grouped[:].bitcast(F32),
-                    pairs_t[:].rearrange("p cpass half s -> p cpass s half"),
+                copy = nc.vector.tensor_copy if lane % 2 == 0 else nc.scalar.copy
+                copy(
+                    out=x_grouped[:].bitcast(F32),
+                    in_=pairs_t[:].rearrange("p cpass half s -> p cpass s half"),
                 )
                 nc.vector.quantize_mx(
                     out=x_codes[:, group, lane, :].bitcast(FP8X4),
@@ -119,57 +114,74 @@ def tile_transformer_block_pa_kernel(tc, x, w_qk_words, w_qk_scales, out):
                     in_=x_grouped[:].rearrange("p cpass s v -> p (cpass s v)"),
                 )
 
-        def project(group, chunk):
+        def project(group, chunk, lanes_first):
             banks = [
-                psum.tile([P, PACK, P], F32, tag="bank", name="lanes%d" % b) for b in range(BANKS_PER_CHUNK)
+                [psum.tile([P, 2, HALF], F32, tag="bank", name="bank%d%d" % (h, u)) for u in range(2)]
+                for h in range(2)
             ]
-            for lane in range(PACK):
-                for b in range(BANKS_PER_CHUNK):
-                    channels = slice(chunk * CHUNK + b * P, chunk * CHUNK + (b + 1) * P)
-                    for cpass in range(CH_PASSES):
-                        positions = slice(cpass * P, (cpass + 1) * P)
-                        nc.tensor.matmul_mx(
-                            out=banks[b][:, lane, :],
-                            lhsT=x_codes[:, group, lane, positions].bitcast(FP8X4),
-                            lhsT_scale=x_scales[:, group, lane, positions],
-                            rhs=w_codes[:, cpass, channels].bitcast(FP8X4),
-                            rhs_scale=w_scales[4 * cpass : P, channels],
-                            start=(cpass == 0),
-                            stop=(cpass == CH_PASSES - 1),
-                        )
+            if lanes_first:
+                order = [(lane, h, cpass) for lane in range(PACK) for h in range(2) for cpass in range(CH_PASSES)]
+            else:
+                order = [(lane, h, cpass) for h in range(2) for lane in range(PACK) for cpass in range(CH_PASSES)]
+            for lane, h, cpass in order:
+                channels = slice(chunk * CHUNK + h * HALF, chunk * CHUNK + (h + 1) * HALF)
+                positions = slice(cpass * P, (cpass + 1) * P)
+                nc.tensor.matmul_mx(
+                    out=banks[h][lane // 2][:, lane % 2, :],
+                    lhsT=x_codes[:, group, lane, positions].bitcast(FP8X4),
+                    lhsT_scale=x_scales[:, group, lane, positions],
+                    rhs=w_codes[:, cpass, channels].bitcast(FP8X4),
+                    rhs_scale=w_scales[4 * cpass : P, channels],
+                    start=(cpass == 0),
+                    stop=(cpass == CH_PASSES - 1),
+                )
             return banks
 
-        def round_and_group(banks):
-            qk_grouped = qk_stage.tile([P, CHUNK, PACK], BF16, align_bytes=64)
-            for b in range(BANKS_PER_CHUNK):
-                copy_out_of_bank(
-                    b,
-                    qk_grouped[:, b * P : (b + 1) * P, :],
-                    banks[b][:].rearrange("p lane n -> p n lane"),
-                )
-            return qk_grouped
+        def round_to_pairs(banks):
+            pairs = qk_pairs.tile([P, 2, CHUNK], F32, align_bytes=64)
+            for h in range(2):
+                for u in range(2):
+                    copy = nc.vector.tensor_copy if (h, u) == (0, 0) else nc.scalar.copy
+                    copy(
+                        out=pairs[:, u, h * HALF : (h + 1) * HALF]
+                        .bitcast(BF16)
+                        .rearrange("p (n lane) -> p n lane", lane=2),
+                        in_=banks[h][u][:].rearrange("p lane n -> p n lane"),
+                    )
+            return pairs
 
-        def quantise_qk(qk_grouped, group, chunk):
+        def join_pairs(pairs):
+            grouped = qk_stage.tile([P, CHUNK, 2], F32, align_bytes=64)
+            nc.vector.tensor_copy(out=grouped[:], in_=pairs[:].rearrange("p u n -> p n u"))
+            return grouped
+
+        def quantise_qk(grouped, group, chunk):
             channels = slice(chunk * CHUNK, (chunk + 1) * CHUNK)
             nc.vector.quantize_mx(
                 out=qk_codes[:, group, channels].bitcast(FP8X4),
                 scales=qk_scales[:, group, channels],
-                in_=qk_grouped[:].rearrange("p n lane -> p (n lane)"),
+                in_=grouped[:].rearrange("p n u -> p (n u)").bitcast(BF16),
             )
 
         transpose_and_quantise_x(0, sort_x(0))
-        not_yet_quantised = None
+        to_join = None
+        to_quantise = None
         for group in range(SEQ_GROUPS):
-            for chunk in range(CHUNKS):
-                banks = project(group, chunk)
-                if not_yet_quantised is not None:
-                    quantise_qk(*not_yet_quantised)
-                not_yet_quantised = (round_and_group(banks), group, chunk)
-                if chunk == 0 and group + 1 < SEQ_GROUPS:
+            for i, chunk in enumerate(CHUNK_ORDER):
+                banks = project(group, chunk, lanes_first=(group == 0 and i == 0))
+                if to_quantise is not None:
+                    quantise_qk(*to_quantise)
+                    to_quantise = None
+                pairs = round_to_pairs(banks)
+                if to_join is not None:
+                    to_quantise = (join_pairs(to_join[0]), to_join[1], to_join[2])
+                to_join = (pairs, group, chunk)
+                if i == 0 and group + 1 < SEQ_GROUPS:
                     next_pairs = sort_x(group + 1)
-                if chunk == 1 and group + 1 < SEQ_GROUPS:
+                if i == 1 and group + 1 < SEQ_GROUPS:
                     transpose_and_quantise_x(group + 1, next_pairs)
-        quantise_qk(*not_yet_quantised)
+        quantise_qk(*to_quantise)
+        quantise_qk(join_pairs(to_join[0]), to_join[1], to_join[2])
 
         for k_half in range(CH // BANK):
             k_channels = slice(CH + k_half * BANK, CH + (k_half + 1) * BANK)

@@ -27,6 +27,8 @@ CHUNK = 512
 HALF = CHUNK // 2
 CHUNK_ORDER = (2, 0, 1, 3)
 
+WARM_UP_MATMULS = 3
+
 FLOPS = 2 * QK * SEQ * CH + 2 * CH * CH * SEQ
 
 
@@ -51,6 +53,12 @@ def tile_transformer_block_pa_kernel(tc, x, w_qk_words, w_qk_scales, out):
         qk_codes = keep.tile([P, SEQ_GROUPS, QK], U32, align_bytes=64)
         qk_scales = keep.tile([P, SEQ_GROUPS, QK], U8, align_bytes=64)
 
+        zeros = keep.tile([P, BANK], BF16)
+        nc.vector.memset(zeros[:], 0.0)
+        unread = psum.tile([P, BANK], F32, tag="bank")
+        for repeat in range(WARM_UP_MATMULS):
+            nc.tensor.matmul(unread[:], lhsT=zeros[:, 0:P], rhs=zeros[:], start=True, stop=True)
+
         nc.vector.memset(w_scales[:].bitcast(I32), 0)
         make_identity(nc, identity[:])
 
@@ -68,19 +76,20 @@ def tile_transformer_block_pa_kernel(tc, x, w_qk_words, w_qk_scales, out):
                     in_=w_qk_scales[:, 4 * quarter : 4 * quarter + 4, :].bitcast(I32),
                 )
 
-        def load_w_codes(chunk):
+        def load_w_codes(first, width):
             nc.sync.dma_start(
-                out=w_codes[:, :, chunk * CHUNK : (chunk + 1) * CHUNK].bitcast(I32),
-                in_=w_bytes[:, :, chunk * CHUNK * PACK : (chunk + 1) * CHUNK * PACK].bitcast(I32),
+                out=w_codes[:, :, first : first + width].bitcast(I32),
+                in_=w_bytes[:, :, first * PACK : (first + width) * PACK].bitcast(I32),
             )
 
         load_x(0)
         load_w_scales()
-        load_w_codes(CHUNK_ORDER[0])
-        load_w_codes(CHUNK_ORDER[1])
+        load_w_codes(CHUNK_ORDER[0] * CHUNK, HALF)
+        load_w_codes(CHUNK_ORDER[0] * CHUNK + HALF, HALF)
+        load_w_codes(CHUNK_ORDER[1] * CHUNK, CHUNK)
         load_x(1)
-        load_w_codes(CHUNK_ORDER[2])
-        load_w_codes(CHUNK_ORDER[3])
+        load_w_codes(CHUNK_ORDER[2] * CHUNK, CHUNK)
+        load_w_codes(CHUNK_ORDER[3] * CHUNK, CHUNK)
         load_x(2)
 
         def sort_x(group):
@@ -92,18 +101,31 @@ def tile_transformer_block_pa_kernel(tc, x, w_qk_words, w_qk_scales, out):
                     .bitcast(F32)
                     .rearrange("p (cpass k half) -> p cpass half k", cpass=CH_PASSES, half=2),
                 )
-            return pairs
+            return [
+                [[pairs[:, lane, cpass, half, :] for half in range(2)] for cpass in range(CH_PASSES)]
+                for lane in range(PACK)
+            ]
 
-        def transpose_and_quantise_x(group, pairs):
+        def leave_x(group):
+            words = [x_rows[:, group, lane, :].bitcast(F32) for lane in range(PACK)]
+            return [
+                [
+                    [words[lane][:, 2 * P * cpass + half : 2 * P * (cpass + 1) : 2] for half in range(2)]
+                    for cpass in range(CH_PASSES)
+                ]
+                for lane in range(PACK)
+            ]
+
+        def transpose_and_quantise_x(group, pairs, vectors_lanes):
             for lane in range(PACK):
                 pairs_t = psum.tile([P, CH_PASSES, 2, P], F32, tag="bank")
                 for cpass in range(CH_PASSES):
                     for half in range(2):
                         nc.tensor.transpose(
-                            pairs_t[:, cpass, half, :], pairs[:, lane, cpass, half, :], identity[:]
+                            pairs_t[:, cpass, half, :], pairs[lane][cpass][half], identity[:]
                         )
                 x_grouped = x_stage.tile([P, CH_PASSES, P, PACK], BF16, align_bytes=64)
-                copy = nc.vector.tensor_copy if lane % 2 == 0 else nc.scalar.copy
+                copy = nc.vector.tensor_copy if lane in vectors_lanes else nc.scalar.copy
                 copy(
                     out=x_grouped[:].bitcast(F32),
                     in_=pairs_t[:].rearrange("p cpass half s -> p cpass s half"),
@@ -114,16 +136,13 @@ def tile_transformer_block_pa_kernel(tc, x, w_qk_words, w_qk_scales, out):
                     in_=x_grouped[:].rearrange("p cpass s v -> p (cpass s v)"),
                 )
 
-        def project(group, chunk, lanes_first):
+        def project(group, chunk):
             banks = [
                 [psum.tile([P, 2, HALF], F32, tag="bank", name="bank%d%d" % (h, u)) for u in range(2)]
                 for h in range(2)
             ]
-            if lanes_first:
-                order = [(lane, h, cpass) for lane in range(PACK) for h in range(2) for cpass in range(CH_PASSES)]
-            else:
-                order = [(lane, h, cpass) for h in range(2) for lane in range(PACK) for cpass in range(CH_PASSES)]
-            for lane, h, cpass in order:
+            order = [(h, lane, cpass) for h in range(2) for lane in range(PACK) for cpass in range(CH_PASSES)]
+            for h, lane, cpass in order:
                 channels = slice(chunk * CHUNK + h * HALF, chunk * CHUNK + (h + 1) * HALF)
                 positions = slice(cpass * P, (cpass + 1) * P)
                 nc.tensor.matmul_mx(
@@ -163,12 +182,12 @@ def tile_transformer_block_pa_kernel(tc, x, w_qk_words, w_qk_scales, out):
                 in_=grouped[:].rearrange("p n u -> p (n u)").bitcast(BF16),
             )
 
-        transpose_and_quantise_x(0, sort_x(0))
+        transpose_and_quantise_x(0, leave_x(0), vectors_lanes=(2,))
         to_join = None
         to_quantise = None
         for group in range(SEQ_GROUPS):
             for i, chunk in enumerate(CHUNK_ORDER):
-                banks = project(group, chunk, lanes_first=(group == 0 and i == 0))
+                banks = project(group, chunk)
                 if to_quantise is not None:
                     quantise_qk(*to_quantise)
                     to_quantise = None
@@ -179,30 +198,32 @@ def tile_transformer_block_pa_kernel(tc, x, w_qk_words, w_qk_scales, out):
                 if i == 0 and group + 1 < SEQ_GROUPS:
                     next_pairs = sort_x(group + 1)
                 if i == 1 and group + 1 < SEQ_GROUPS:
-                    transpose_and_quantise_x(group + 1, next_pairs)
+                    transpose_and_quantise_x(group + 1, next_pairs, vectors_lanes=(0, 2))
         quantise_qk(*to_quantise)
         quantise_qk(join_pairs(to_join[0]), to_join[1], to_join[2])
 
+        scalars_turn = True
         for k_half in range(CH // BANK):
-            k_channels = slice(CH + k_half * BANK, CH + (k_half + 1) * BANK)
             for q_tile in range(CH // P):
                 q_channels = slice(q_tile * P, (q_tile + 1) * P)
-                sums = psum.tile([P, BANK], F32, tag="bank")
-                for group in range(SEQ_GROUPS):
-                    nc.tensor.matmul_mx(
-                        out=sums[:],
-                        lhsT=qk_codes[:, group, q_channels].bitcast(FP8X4),
-                        lhsT_scale=qk_scales[:, group, q_channels],
-                        rhs=qk_codes[:, group, k_channels].bitcast(FP8X4),
-                        rhs_scale=qk_scales[:, group, k_channels],
-                        start=(group == 0),
-                        stop=(group == SEQ_GROUPS - 1),
-                    )
-                score = out_stage.tile([P, BANK], F32)
-                if q_tile % 2 == 0:
-                    nc.scalar.mul(out=score[:], in_=sums[:], mul=1.0 / math.sqrt(SEQ))
-                else:
-                    nc.vector.tensor_scalar_mul(out=score[:], in0=sums[:], scalar1=1.0 / math.sqrt(SEQ))
-                nc.sync.dma_start(
-                    out=out[0, q_channels, k_half * BANK : (k_half + 1) * BANK], in_=score[:]
-                )
+                last = k_half == CH // BANK - 1 and q_tile == CH // P - 1
+                width = BANK // 2 if last else BANK
+                for first in range(k_half * BANK, (k_half + 1) * BANK, width):
+                    sums = psum.tile([P, width], F32, tag="bank")
+                    for group in range(SEQ_GROUPS):
+                        nc.tensor.matmul_mx(
+                            out=sums[:],
+                            lhsT=qk_codes[:, group, q_channels].bitcast(FP8X4),
+                            lhsT_scale=qk_scales[:, group, q_channels],
+                            rhs=qk_codes[:, group, CH + first : CH + first + width].bitcast(FP8X4),
+                            rhs_scale=qk_scales[:, group, CH + first : CH + first + width],
+                            start=(group == 0),
+                            stop=(group == SEQ_GROUPS - 1),
+                        )
+                    score = out_stage.tile([P, width], F32)
+                    if scalars_turn:
+                        nc.scalar.mul(out=score[:], in_=sums[:], mul=1.0 / math.sqrt(SEQ))
+                    else:
+                        nc.vector.tensor_scalar_mul(out=score[:], in0=sums[:], scalar1=1.0 / math.sqrt(SEQ))
+                    scalars_turn = not scalars_turn
+                    nc.sync.dma_start(out=out[0, q_channels, first : first + width], in_=score[:])

@@ -198,7 +198,7 @@ def tile_transformer_block_pa_kernel(tc, x, w_qk_words, w_qk_scales, out):
                 if i == 0 and group + 1 < SEQ_GROUPS:
                     next_pairs = sort_x(group + 1)
                 if i == 1 and group + 1 < SEQ_GROUPS:
-                    transpose_and_quantise_x(group + 1, next_pairs, vectors_lanes=(0, 2))
+                    transpose_and_quantise_x(group + 1, next_pairs, vectors_lanes=())
         quantise_qk(*to_quantise)
         quantise_qk(join_pairs(to_join[0]), to_join[1], to_join[2])
 

@@ -116,7 +116,8 @@ def tile_transformer_block_pa_kernel(tc, x, w_qk_words, w_qk_scales, out):
                 for lane in range(PACK)
             ]
 
-        def transpose_and_quantise_x(group, pairs, vectors_lanes):
+        def transpose_x(pairs):
+            grouped = []
             for lane in range(PACK):
                 pairs_t = psum.tile([P, CH_PASSES, 2, P], F32, tag="bank")
                 for cpass in range(CH_PASSES):
@@ -125,15 +126,19 @@ def tile_transformer_block_pa_kernel(tc, x, w_qk_words, w_qk_scales, out):
                             pairs_t[:, cpass, half, :], pairs[lane][cpass][half], identity[:]
                         )
                 x_grouped = x_stage.tile([P, CH_PASSES, P, PACK], BF16, align_bytes=64)
-                copy = nc.vector.tensor_copy if lane in vectors_lanes else nc.scalar.copy
-                copy(
+                nc.scalar.copy(
                     out=x_grouped[:].bitcast(F32),
                     in_=pairs_t[:].rearrange("p cpass half s -> p cpass s half"),
                 )
+                grouped.append(x_grouped)
+            return grouped
+
+        def quantise_x(grouped, group):
+            for lane in range(PACK):
                 nc.vector.quantize_mx(
                     out=x_codes[:, group, lane, :].bitcast(FP8X4),
                     scales=x_scales[:, group, lane, :],
-                    in_=x_grouped[:].rearrange("p cpass s v -> p (cpass s v)"),
+                    in_=grouped[lane][:].rearrange("p cpass s v -> p (cpass s v)"),
                 )
 
         def project(group, chunk):
@@ -141,8 +146,10 @@ def tile_transformer_block_pa_kernel(tc, x, w_qk_words, w_qk_scales, out):
                 [psum.tile([P, 2, HALF], F32, tag="bank", name="bank%d%d" % (h, u)) for u in range(2)]
                 for h in range(2)
             ]
-            order = [(h, lane, cpass) for h in range(2) for lane in range(PACK) for cpass in range(CH_PASSES)]
-            for h, lane, cpass in order:
+            order = [(h, lane) for h in range(2) for lane in range(PACK)]
+            if (group, chunk) == (0, CHUNK_ORDER[0]):
+                order = sorted(order, key=lambda h_lane: h_lane[1] + 2.5 * h_lane[0])
+            for h, lane, cpass in [(h, lane, cpass) for h, lane in order for cpass in range(CH_PASSES)]:
                 channels = slice(chunk * CHUNK + h * HALF, chunk * CHUNK + (h + 1) * HALF)
                 positions = slice(cpass * P, (cpass + 1) * P)
                 nc.tensor.matmul_mx(
@@ -182,7 +189,7 @@ def tile_transformer_block_pa_kernel(tc, x, w_qk_words, w_qk_scales, out):
                 in_=grouped[:].rearrange("p n u -> p (n u)").bitcast(BF16),
             )
 
-        transpose_and_quantise_x(0, leave_x(0), vectors_lanes=(2,))
+        quantise_x(transpose_x(leave_x(0)), 0)
         to_join = None
         to_quantise = None
         for group in range(SEQ_GROUPS):
@@ -198,7 +205,9 @@ def tile_transformer_block_pa_kernel(tc, x, w_qk_words, w_qk_scales, out):
                 if i == 0 and group + 1 < SEQ_GROUPS:
                     next_pairs = sort_x(group + 1)
                 if i == 1 and group + 1 < SEQ_GROUPS:
-                    transpose_and_quantise_x(group + 1, next_pairs, vectors_lanes=())
+                    next_x = transpose_x(next_pairs)
+                if i == 2 and group + 1 < SEQ_GROUPS:
+                    quantise_x(next_x, group + 1)
         quantise_qk(*to_quantise)
         quantise_qk(join_pairs(to_join[0]), to_join[1], to_join[2])
 

@@ -55,9 +55,13 @@ def tile_transformer_block_pa_kernel(tc, x, w_qk_words, w_qk_scales, out):
 
         zeros = keep.tile([P, BANK], BF16)
         nc.vector.memset(zeros[:], 0.0)
-        unread = psum.tile([P, BANK], F32, tag="bank")
-        for repeat in range(WARM_UP_MATMULS):
-            nc.tensor.matmul(unread[:], lhsT=zeros[:, 0:P], rhs=zeros[:], start=True, stop=True)
+        unread = psum.tile([P, BANK], F32, tag="bank", name="unread")
+
+        def multiply_zeros(times):
+            for repeat in range(times):
+                nc.tensor.matmul(unread[:], lhsT=zeros[:, 0:P], rhs=zeros[:], start=True, stop=True)
+
+        multiply_zeros(WARM_UP_MATMULS)
 
         nc.vector.memset(w_scales[:].bitcast(I32), 0)
         make_identity(nc, identity[:])
@@ -116,7 +120,7 @@ def tile_transformer_block_pa_kernel(tc, x, w_qk_words, w_qk_scales, out):
                 for lane in range(PACK)
             ]
 
-        def transpose_x(pairs):
+        def transpose_x(pairs, zeros_between):
             grouped = []
             for lane in range(PACK):
                 pairs_t = psum.tile([P, CH_PASSES, 2, P], F32, tag="bank")
@@ -125,6 +129,7 @@ def tile_transformer_block_pa_kernel(tc, x, w_qk_words, w_qk_scales, out):
                         nc.tensor.transpose(
                             pairs_t[:, cpass, half, :], pairs[lane][cpass][half], identity[:]
                         )
+                multiply_zeros(zeros_between)
                 x_grouped = x_stage.tile([P, CH_PASSES, P, PACK], BF16, align_bytes=64)
                 nc.scalar.copy(
                     out=x_grouped[:].bitcast(F32),
@@ -189,7 +194,7 @@ def tile_transformer_block_pa_kernel(tc, x, w_qk_words, w_qk_scales, out):
                 in_=grouped[:].rearrange("p n u -> p (n u)").bitcast(BF16),
             )
 
-        quantise_x(transpose_x(leave_x(0)), 0)
+        quantise_x(transpose_x(leave_x(0), zeros_between=1), 0)
         to_join = None
         to_quantise = None
         for group in range(SEQ_GROUPS):
@@ -205,7 +210,7 @@ def tile_transformer_block_pa_kernel(tc, x, w_qk_words, w_qk_scales, out):
                 if i == 0 and group + 1 < SEQ_GROUPS:
                     next_pairs = sort_x(group + 1)
                 if i == 1 and group + 1 < SEQ_GROUPS:
-                    next_x = transpose_x(next_pairs)
+                    next_x = transpose_x(next_pairs, zeros_between=0)
                 if i == 2 and group + 1 < SEQ_GROUPS:
                     quantise_x(next_x, group + 1)
         quantise_qk(*to_quantise)

@@ -27,7 +27,7 @@ CHUNK = 512
 HALF = CHUNK // 2
 CHUNK_ORDER = (2, 0, 1, 3)
 
-WARM_UP_MATMULS = 3
+WARM_UP_MATMULS = 5
 
 FLOPS = 2 * QK * SEQ * CH + 2 * CH * CH * SEQ
 
@@ -54,7 +54,7 @@ def tile_transformer_block_pa_kernel(tc, x, w_qk_words, w_qk_scales, out):
         qk_scales = keep.tile([P, SEQ_GROUPS, QK], U8, align_bytes=64)
 
         zeros = keep.tile([P, BANK], BF16)
-        nc.vector.memset(zeros[:], 0.0)
+        nc.vector.memset(zeros[:].bitcast(F32), 0.0)
         unread = psum.tile([P, BANK], F32, tag="bank", name="unread")
 
         def multiply_zeros(times):
@@ -105,20 +105,7 @@ def tile_transformer_block_pa_kernel(tc, x, w_qk_words, w_qk_scales, out):
                     .bitcast(F32)
                     .rearrange("p (cpass k half) -> p cpass half k", cpass=CH_PASSES, half=2),
                 )
-            return [
-                [[pairs[:, lane, cpass, half, :] for half in range(2)] for cpass in range(CH_PASSES)]
-                for lane in range(PACK)
-            ]
-
-        def leave_x(group):
-            words = [x_rows[:, group, lane, :].bitcast(F32) for lane in range(PACK)]
-            return [
-                [
-                    [words[lane][:, 2 * P * cpass + half : 2 * P * (cpass + 1) : 2] for half in range(2)]
-                    for cpass in range(CH_PASSES)
-                ]
-                for lane in range(PACK)
-            ]
+            return pairs
 
         def transpose_x(pairs, zeros_between):
             grouped = []
@@ -127,7 +114,7 @@ def tile_transformer_block_pa_kernel(tc, x, w_qk_words, w_qk_scales, out):
                 for cpass in range(CH_PASSES):
                     for half in range(2):
                         nc.tensor.transpose(
-                            pairs_t[:, cpass, half, :], pairs[lane][cpass][half], identity[:]
+                            pairs_t[:, cpass, half, :], pairs[:, lane, cpass, half, :], identity[:]
                         )
                 multiply_zeros(zeros_between)
                 x_grouped = x_stage.tile([P, CH_PASSES, P, PACK], BF16, align_bytes=64)
@@ -194,7 +181,7 @@ def tile_transformer_block_pa_kernel(tc, x, w_qk_words, w_qk_scales, out):
                 in_=grouped[:].rearrange("p n u -> p (n u)").bitcast(BF16),
             )
 
-        quantise_x(transpose_x(leave_x(0), zeros_between=1), 0)
+        quantise_x(transpose_x(sort_x(0), zeros_between=1), 0)
         to_join = None
         to_quantise = None
         for group in range(SEQ_GROUPS):
@@ -221,8 +208,8 @@ def tile_transformer_block_pa_kernel(tc, x, w_qk_words, w_qk_scales, out):
             for q_tile in range(CH // P):
                 q_channels = slice(q_tile * P, (q_tile + 1) * P)
                 last = k_half == CH // BANK - 1 and q_tile == CH // P - 1
-                width = BANK // 2 if last else BANK
-                for first in range(k_half * BANK, (k_half + 1) * BANK, width):
+                first = k_half * BANK
+                for width in (BANK // 2, BANK // 4, BANK // 4) if last else (BANK,):
                     sums = psum.tile([P, width], F32, tag="bank")
                     for group in range(SEQ_GROUPS):
                         nc.tensor.matmul_mx(
@@ -241,3 +228,4 @@ def tile_transformer_block_pa_kernel(tc, x, w_qk_words, w_qk_scales, out):
                         nc.vector.tensor_scalar_mul(out=score[:], in0=sums[:], scalar1=1.0 / math.sqrt(SEQ))
                     scalars_turn = not scalars_turn
                     nc.sync.dma_start(out=out[0, q_channels, first : first + width], in_=score[:])
+                    first += width

@@ -25,7 +25,7 @@ CH_PASSES = CH // K_PASS
 SEQ_GROUPS = SEQ // K_PASS
 CHUNK = 512
 HALF = CHUNK // 2
-CHUNK_ORDER = (2, 0, 1, 3)
+CHUNK_ORDER = (2, 0, 3, 1)
 
 WARM_UP_MATMULS = 5
 
@@ -73,11 +73,12 @@ def tile_transformer_block_pa_kernel(tc, x, w_qk_words, w_qk_scales, out):
             for lane in range(PACK):
                 nc.sync.dma_start(out=x_rows[:, group, lane, :], in_=x_by_lane[group, :, lane, :])
 
-        def load_w_scales():
+        def load_w_scales(chunk):
+            columns = slice(chunk * CHUNK, (chunk + 1) * CHUNK)
             for quarter in range(4):
                 nc.sync.dma_start(
-                    out=w_scales[32 * quarter : 32 * quarter + 4 * CH_PASSES, :].bitcast(I32),
-                    in_=w_qk_scales[:, 4 * quarter : 4 * quarter + 4, :].bitcast(I32),
+                    out=w_scales[32 * quarter : 32 * quarter + 4 * CH_PASSES, columns].bitcast(I32),
+                    in_=w_qk_scales[:, 4 * quarter : 4 * quarter + 4, columns].bitcast(I32),
                 )
 
         def load_w_codes(first, width):
@@ -87,13 +88,16 @@ def tile_transformer_block_pa_kernel(tc, x, w_qk_words, w_qk_scales, out):
             )
 
         load_x(0)
-        load_w_scales()
+        load_w_scales(CHUNK_ORDER[0])
         load_w_codes(CHUNK_ORDER[0] * CHUNK, HALF)
         load_w_codes(CHUNK_ORDER[0] * CHUNK + HALF, HALF)
         load_w_codes(CHUNK_ORDER[1] * CHUNK, CHUNK)
+        load_w_scales(CHUNK_ORDER[1])
         load_x(1)
         load_w_codes(CHUNK_ORDER[2] * CHUNK, CHUNK)
+        load_w_scales(CHUNK_ORDER[2])
         load_w_codes(CHUNK_ORDER[3] * CHUNK, CHUNK)
+        load_w_scales(CHUNK_ORDER[3])
         load_x(2)
 
         def sort_x(group):
@@ -203,29 +207,33 @@ def tile_transformer_block_pa_kernel(tc, x, w_qk_words, w_qk_scales, out):
         quantise_qk(*to_quantise)
         quantise_qk(join_pairs(to_join[0]), to_join[1], to_join[2])
 
+        tiles = [
+            (q_half * CH // 2 + q_tile * P, k_half * BANK)
+            for q_half in range(2)
+            for k_half in range(CH // BANK)
+            for q_tile in range(CH // 2 // P)
+        ]
         scalars_turn = True
-        for k_half in range(CH // BANK):
-            for q_tile in range(CH // P):
-                q_channels = slice(q_tile * P, (q_tile + 1) * P)
-                last = k_half == CH // BANK - 1 and q_tile == CH // P - 1
-                first = k_half * BANK
-                for width in (BANK // 2, BANK // 4, BANK // 4) if last else (BANK,):
-                    sums = psum.tile([P, width], F32, tag="bank")
-                    for group in range(SEQ_GROUPS):
-                        nc.tensor.matmul_mx(
-                            out=sums[:],
-                            lhsT=qk_codes[:, group, q_channels].bitcast(FP8X4),
-                            lhsT_scale=qk_scales[:, group, q_channels],
-                            rhs=qk_codes[:, group, CH + first : CH + first + width].bitcast(FP8X4),
-                            rhs_scale=qk_scales[:, group, CH + first : CH + first + width],
-                            start=(group == 0),
-                            stop=(group == SEQ_GROUPS - 1),
-                        )
-                    score = out_stage.tile([P, width], F32)
-                    if scalars_turn:
-                        nc.scalar.mul(out=score[:], in_=sums[:], mul=1.0 / math.sqrt(SEQ))
-                    else:
-                        nc.vector.tensor_scalar_mul(out=score[:], in0=sums[:], scalar1=1.0 / math.sqrt(SEQ))
-                    scalars_turn = not scalars_turn
-                    nc.sync.dma_start(out=out[0, q_channels, first : first + width], in_=score[:])
-                    first += width
+        for q_first, first in tiles:
+            q_channels = slice(q_first, q_first + P)
+            last = (q_first, first) == tiles[-1]
+            for width in (BANK // 2, BANK // 4, BANK // 4) if last else (BANK,):
+                sums = psum.tile([P, width], F32, tag="bank")
+                for group in range(SEQ_GROUPS):
+                    nc.tensor.matmul_mx(
+                        out=sums[:],
+                        lhsT=qk_codes[:, group, q_channels].bitcast(FP8X4),
+                        lhsT_scale=qk_scales[:, group, q_channels],
+                        rhs=qk_codes[:, group, CH + first : CH + first + width].bitcast(FP8X4),
+                        rhs_scale=qk_scales[:, group, CH + first : CH + first + width],
+                        start=(group == 0),
+                        stop=(group == SEQ_GROUPS - 1),
+                    )
+                score = out_stage.tile([P, width], F32)
+                if scalars_turn:
+                    nc.scalar.mul(out=score[:], in_=sums[:], mul=1.0 / math.sqrt(SEQ))
+                else:
+                    nc.vector.tensor_scalar_mul(out=score[:], in0=sums[:], scalar1=1.0 / math.sqrt(SEQ))
+                scalars_turn = not scalars_turn
+                nc.sync.dma_start(out=out[0, q_channels, first : first + width], in_=score[:])
+                first += width

@@ -88,8 +88,8 @@ def tile_transformer_block_pa_kernel(tc, x, w_qk_words, w_qk_scales, out):
             )
 
         load_x(0)
-        load_w_scales(CHUNK_ORDER[0])
         load_w_codes(CHUNK_ORDER[0] * CHUNK, HALF)
+        load_w_scales(CHUNK_ORDER[0])
         load_w_codes(CHUNK_ORDER[0] * CHUNK + HALF, HALF)
         load_w_codes(CHUNK_ORDER[1] * CHUNK, CHUNK)
         load_w_scales(CHUNK_ORDER[1])

@@ -27,7 +27,7 @@ CHUNK = 512
 HALF = CHUNK // 2
 CHUNK_ORDER = (2, 0, 3, 1)
 
-WARM_UP_MATMULS = 5
+WARM_UP_MATMULS = 4
 
 FLOPS = 2 * QK * SEQ * CH + 2 * CH * CH * SEQ
 
@@ -120,7 +120,8 @@ def tile_transformer_block_pa_kernel(tc, x, w_qk_words, w_qk_scales, out):
                         nc.tensor.transpose(
                             pairs_t[:, cpass, half, :], pairs[:, lane, cpass, half, :], identity[:]
                         )
-                multiply_zeros(zeros_between)
+                if lane < PACK - 1:
+                    multiply_zeros(zeros_between)
                 x_grouped = x_stage.tile([P, CH_PASSES, P, PACK], BF16, align_bytes=64)
                 nc.scalar.copy(
                     out=x_grouped[:].bitcast(F32),
@@ -144,7 +145,7 @@ def tile_transformer_block_pa_kernel(tc, x, w_qk_words, w_qk_scales, out):
             ]
             order = [(h, lane) for h in range(2) for lane in range(PACK)]
             if (group, chunk) == (0, CHUNK_ORDER[0]):
-                order = sorted(order, key=lambda h_lane: h_lane[1] + 2.5 * h_lane[0])
+                order = sorted(order, key=lambda h_lane: h_lane[1] + 1.5 * h_lane[0])
             for h, lane, cpass in [(h, lane, cpass) for h, lane in order for cpass in range(CH_PASSES)]:
                 channels = slice(chunk * CHUNK + h * HALF, chunk * CHUNK + (h + 1) * HALF)
                 positions = slice(cpass * P, (cpass + 1) * P)

@@ -27,6 +27,10 @@ CHUNK = 512
 HALF = CHUNK // 2
 CHUNK_ORDER = (2, 0, 3, 1)
 
+FIRST_COLUMNS = slice(CHUNK_ORDER[0] * CHUNK, CHUNK_ORDER[0] * CHUNK + CHUNK)
+BEFORE_FIRST = slice(0, FIRST_COLUMNS.start)
+BEHIND_FIRST = slice(FIRST_COLUMNS.stop, QK)
+
 WARM_UP_MATMULS = 4
 
 FLOPS = 2 * QK * SEQ * CH + 2 * CH * CH * SEQ
@@ -54,6 +58,7 @@ def tile_transformer_block_pa_kernel(tc, x, w_qk_words, w_qk_scales, out):
         qk_scales = keep.tile([P, SEQ_GROUPS, QK], U8, align_bytes=64)
 
         zeros = keep.tile([P, BANK], BF16)
+        nc.vector.memset(w_scales[:, FIRST_COLUMNS].bitcast(I32), 0)
         nc.vector.memset(zeros[:].bitcast(F32), 0.0)
         unread = psum.tile([P, BANK], F32, tag="bank", name="unread")
 
@@ -63,18 +68,21 @@ def tile_transformer_block_pa_kernel(tc, x, w_qk_words, w_qk_scales, out):
 
         multiply_zeros(WARM_UP_MATMULS)
 
-        nc.vector.memset(w_scales[:].bitcast(I32), 0)
+        nc.vector.memset(w_scales[:, BEFORE_FIRST].bitcast(I32), 0)
+        nc.vector.memset(w_scales[:, BEHIND_FIRST].bitcast(I32), 0)
         make_identity(nc, identity[:])
 
-        x_by_lane = x[0].rearrange("(group p lane) c -> group p lane c", p=P, lane=PACK)
+        x_by_group = x[0].rearrange("(group p lane) c -> group p (lane c)", p=P, lane=PACK)
         w_bytes = w_qk_words.rearrange("cpass p n v -> p cpass (n v)")
 
-        def load_x(group):
-            for lane in range(PACK):
-                nc.sync.dma_start(out=x_rows[:, group, lane, :], in_=x_by_lane[group, :, lane, :])
+        def load_x(group, first_lane, lanes):
+            columns = slice(first_lane * CH, (first_lane + lanes) * CH)
+            nc.sync.dma_start(
+                out=x_rows[:, group, :, :].rearrange("p lane c -> p (lane c)")[:, columns],
+                in_=x_by_group[group, :, columns],
+            )
 
-        def load_w_scales(chunk):
-            columns = slice(chunk * CHUNK, (chunk + 1) * CHUNK)
+        def load_w_scales(columns):
             for quarter in range(4):
                 nc.sync.dma_start(
                     out=w_scales[32 * quarter : 32 * quarter + 4 * CH_PASSES, columns].bitcast(I32),
@@ -87,18 +95,21 @@ def tile_transformer_block_pa_kernel(tc, x, w_qk_words, w_qk_scales, out):
                 in_=w_bytes[:, :, first * PACK : (first + width) * PACK].bitcast(I32),
             )
 
-        load_x(0)
+        load_x(0, 0, 1)
+        load_x(0, 1, 1)
+        load_w_scales(FIRST_COLUMNS)
+        load_x(0, 2, 1)
+        load_x(0, 3, 1)
         load_w_codes(CHUNK_ORDER[0] * CHUNK, HALF)
-        load_w_scales(CHUNK_ORDER[0])
         load_w_codes(CHUNK_ORDER[0] * CHUNK + HALF, HALF)
         load_w_codes(CHUNK_ORDER[1] * CHUNK, CHUNK)
-        load_w_scales(CHUNK_ORDER[1])
-        load_x(1)
+        load_w_scales(BEFORE_FIRST)
+        load_x(1, 0, 2)
+        load_x(1, 2, 2)
         load_w_codes(CHUNK_ORDER[2] * CHUNK, CHUNK)
-        load_w_scales(CHUNK_ORDER[2])
+        load_w_scales(BEHIND_FIRST)
         load_w_codes(CHUNK_ORDER[3] * CHUNK, CHUNK)
-        load_w_scales(CHUNK_ORDER[3])
-        load_x(2)
+        load_x(2, 0, PACK)
 
         def sort_x(group):
             pairs = x_sort.tile([P, PACK, CH_PASSES, 2, P], F32)

@@ -44,7 +44,7 @@ def tile_transformer_block_pa_kernel(tc, x, w_qk_words, w_qk_scales, out):
         x_stage = ctx.enter_context(tc.tile_pool(name="x_stage", bufs=4))
         qk_pairs = ctx.enter_context(tc.tile_pool(name="qk_pairs", bufs=3))
         qk_stage = ctx.enter_context(tc.tile_pool(name="qk_stage", bufs=3))
-        out_stage = ctx.enter_context(tc.tile_pool(name="out_stage", bufs=16))
+        out_stage = ctx.enter_context(tc.tile_pool(name="out_stage", bufs=8))
         psum = ctx.enter_context(tc.psum_pool(name="psum", bufs=PSUM_BANKS))
         ctx.enter_context(tc.manual_schedule())
 
@@ -219,33 +219,42 @@ def tile_transformer_block_pa_kernel(tc, x, w_qk_words, w_qk_scales, out):
         quantise_qk(*to_quantise)
         quantise_qk(join_pairs(to_join[0]), to_join[1], to_join[2])
 
-        tiles = [
-            (q_half * CH // 2 + q_tile * P, k_half * BANK)
-            for q_half in range(2)
-            for k_half in range(CH // BANK)
-            for q_tile in range(CH // 2 // P)
-        ]
-        scalars_turn = True
-        for q_first, first in tiles:
+        def multiply_qk(q_channels, first, width, score, scale):
+            sums = psum.tile([P, width], F32, tag="bank")
+            for group in range(SEQ_GROUPS):
+                nc.tensor.matmul_mx(
+                    out=sums[:],
+                    lhsT=qk_codes[:, group, q_channels].bitcast(FP8X4),
+                    lhsT_scale=qk_scales[:, group, q_channels],
+                    rhs=qk_codes[:, group, CH + first : CH + first + width].bitcast(FP8X4),
+                    rhs_scale=qk_scales[:, group, CH + first : CH + first + width],
+                    start=(group == 0),
+                    stop=(group == SEQ_GROUPS - 1),
+                )
+            scale(score, sums[:])
+
+        def scale_on_scalar(score, sums):
+            nc.scalar.mul(out=score, in_=sums, mul=1.0 / math.sqrt(SEQ))
+
+        def scale_on_vector(score, sums):
+            nc.vector.tensor_scalar_mul(out=score, in0=sums, scalar1=1.0 / math.sqrt(SEQ))
+
+        for q_first in range(0, CH, P):
             q_channels = slice(q_first, q_first + P)
-            last = (q_first, first) == tiles[-1]
-            for width in (BANK // 2, BANK // 4, BANK // 4) if last else (BANK,):
-                sums = psum.tile([P, width], F32, tag="bank")
-                for group in range(SEQ_GROUPS):
-                    nc.tensor.matmul_mx(
-                        out=sums[:],
-                        lhsT=qk_codes[:, group, q_channels].bitcast(FP8X4),
-                        lhsT_scale=qk_scales[:, group, q_channels],
-                        rhs=qk_codes[:, group, CH + first : CH + first + width].bitcast(FP8X4),
-                        rhs_scale=qk_scales[:, group, CH + first : CH + first + width],
-                        start=(group == 0),
-                        stop=(group == SEQ_GROUPS - 1),
-                    )
-                score = out_stage.tile([P, width], F32)
-                if scalars_turn:
-                    nc.scalar.mul(out=score[:], in_=sums[:], mul=1.0 / math.sqrt(SEQ))
-                else:
-                    nc.vector.tensor_scalar_mul(out=score[:], in0=sums[:], scalar1=1.0 / math.sqrt(SEQ))
-                scalars_turn = not scalars_turn
-                nc.sync.dma_start(out=out[0, q_channels, first : first + width], in_=score[:])
-                first += width
+            if q_first + P < CH:
+                score = out_stage.tile([P, CH], F32)
+                multiply_qk(q_channels, 0, BANK, score[:, 0:BANK], scale_on_scalar)
+                multiply_qk(q_channels, BANK, BANK, score[:, BANK:CH], scale_on_vector)
+                nc.sync.dma_start(out=out[0, q_channels, :], in_=score[:])
+            else:
+                first = 0
+                for width, scale in (
+                    (BANK, scale_on_scalar),
+                    (BANK // 2, scale_on_vector),
+                    (BANK // 4, scale_on_scalar),
+                    (BANK // 4, scale_on_vector),
+                ):
+                    piece = out_stage.tile([P, width], F32)
+                    multiply_qk(q_channels, first, width, piece[:], scale)
+                    nc.sync.dma_start(out=out[0, q_channels, first : first + width], in_=piece[:])
+                    first += width

@@ -111,16 +111,17 @@ def tile_transformer_block_pa_kernel(tc, x, w_qk_words, w_qk_scales, out):
         load_w_codes(CHUNK_ORDER[3] * CHUNK, CHUNK)
         load_x(2, 0, PACK)
 
-        def sort_x(group):
+        def words_by_half(group, lane):
+            words = x_rows[:, group, lane, :].bitcast(F32)
+            return words.rearrange("p (cpass k half) -> p cpass half k", cpass=CH_PASSES, half=2)
+
+        def sort_x(group, lanes):
             pairs = x_sort.tile([P, PACK, CH_PASSES, 2, P], F32)
-            for lane in range(PACK):
-                nc.vector.tensor_copy(
-                    out=pairs[:, lane, :, :, :],
-                    in_=x_rows[:, group, lane, :]
-                    .bitcast(F32)
-                    .rearrange("p (cpass k half) -> p cpass half k", cpass=CH_PASSES, half=2),
-                )
-            return pairs
+            for lane in lanes:
+                nc.vector.tensor_copy(out=pairs[:, lane, :, :, :], in_=words_by_half(group, lane))
+            return [
+                pairs[:, lane, :, :, :] if lane in lanes else words_by_half(group, lane) for lane in range(PACK)
+            ]
 
         def transpose_x(pairs, zeros_between):
             grouped = []
@@ -129,7 +130,7 @@ def tile_transformer_block_pa_kernel(tc, x, w_qk_words, w_qk_scales, out):
                 for cpass in range(CH_PASSES):
                     for half in range(2):
                         nc.tensor.transpose(
-                            pairs_t[:, cpass, half, :], pairs[:, lane, cpass, half, :], identity[:]
+                            pairs_t[:, cpass, half, :], pairs[lane][:, cpass, half, :], identity[:]
                         )
                 if lane < PACK - 1:
                     multiply_zeros(zeros_between)
@@ -197,7 +198,7 @@ def tile_transformer_block_pa_kernel(tc, x, w_qk_words, w_qk_scales, out):
                 in_=grouped[:].rearrange("p n u -> p (n u)").bitcast(BF16),
             )
 
-        quantise_x(transpose_x(sort_x(0), zeros_between=1), 0)
+        quantise_x(transpose_x(sort_x(0, range(1, PACK - 1)), zeros_between=1), 0)
         to_join = None
         to_quantise = None
         for group in range(SEQ_GROUPS):
@@ -211,7 +212,7 @@ def tile_transformer_block_pa_kernel(tc, x, w_qk_words, w_qk_scales, out):
                     to_quantise = (join_pairs(to_join[0]), to_join[1], to_join[2])
                 to_join = (pairs, group, chunk)
                 if i == 0 and group + 1 < SEQ_GROUPS:
-                    next_pairs = sort_x(group + 1)
+                    next_pairs = sort_x(group + 1, range(PACK))
                 if i == 1 and group + 1 < SEQ_GROUPS:
                     next_x = transpose_x(next_pairs, zeros_between=0)
                 if i == 2 and group + 1 < SEQ_GROUPS:
@@ -245,7 +246,8 @@ def tile_transformer_block_pa_kernel(tc, x, w_qk_words, w_qk_scales, out):
                 score = out_stage.tile([P, CH], F32)
                 multiply_qk(q_channels, 0, BANK, score[:, 0:BANK], scale_on_scalar)
                 multiply_qk(q_channels, BANK, BANK, score[:, BANK:CH], scale_on_vector)
-                nc.sync.dma_start(out=out[0, q_channels, :], in_=score[:])
+                for columns in [slice(0, CH)] if q_first + 2 * P < CH else [slice(0, BANK), slice(BANK, CH)]:
+                    nc.sync.dma_start(out=out[0, q_channels, columns], in_=score[:, columns])
             else:
                 first = 0
                 for width, scale in (

@@ -31,6 +31,9 @@ FIRST_COLUMNS = slice(CHUNK_ORDER[0] * CHUNK, CHUNK_ORDER[0] * CHUNK + CHUNK)
 BEFORE_FIRST = slice(0, FIRST_COLUMNS.start)
 BEHIND_FIRST = slice(FIRST_COLUMNS.stop, QK)
 
+SCALE_STEP = 256
+SCALE_BYTES = slice(SCALE_STEP // 2, SCALE_STEP)
+
 WARM_UP_MATMULS = 4
 
 FLOPS = 2 * QK * SEQ * CH + 2 * CH * CH * SEQ
@@ -51,11 +54,12 @@ def tile_transformer_block_pa_kernel(tc, x, w_qk_words, w_qk_scales, out):
         identity = keep.tile([P, P], F32)
         x_rows = keep.tile([P, SEQ_GROUPS, PACK, CH], BF16)
         x_codes = keep.tile([P, SEQ_GROUPS, PACK, CH_PASSES * P], U32, align_bytes=64)
-        x_scales = keep.tile([P, SEQ_GROUPS, PACK, CH_PASSES * P], U8, align_bytes=64)
+        x_scales = keep.tile([P, SEQ_GROUPS, PACK, CH_PASSES, SCALE_STEP], U8, align_bytes=SCALE_STEP)
         w_codes = keep.tile([P, CH_PASSES, QK], U32, align_bytes=64)
         w_scales = keep.tile([P, QK], U8, align_bytes=64)
         qk_codes = keep.tile([P, SEQ_GROUPS, QK], U32, align_bytes=64)
-        qk_scales = keep.tile([P, SEQ_GROUPS, QK], U8, align_bytes=64)
+        q_scales = keep.tile([P, SEQ_GROUPS, CH // P, SCALE_STEP], U8, align_bytes=SCALE_STEP)
+        k_scales = keep.tile([P, SEQ_GROUPS, CH], U8, align_bytes=SCALE_STEP)
 
         zeros = keep.tile([P, BANK], BF16)
         nc.vector.memset(w_scales[:, FIRST_COLUMNS].bitcast(I32), 0)
@@ -144,11 +148,12 @@ def tile_transformer_block_pa_kernel(tc, x, w_qk_words, w_qk_scales, out):
 
         def quantise_x(grouped, group):
             for lane in range(PACK):
-                nc.vector.quantize_mx(
-                    out=x_codes[:, group, lane, :].bitcast(FP8X4),
-                    scales=x_scales[:, group, lane, :],
-                    in_=grouped[lane][:].rearrange("p cpass s v -> p (cpass s v)"),
-                )
+                for cpass in range(CH_PASSES):
+                    nc.vector.quantize_mx(
+                        out=x_codes[:, group, lane, cpass * P : (cpass + 1) * P].bitcast(FP8X4),
+                        scales=x_scales[:, group, lane, cpass, SCALE_BYTES],
+                        in_=grouped[lane][:, cpass, :, :].rearrange("p s v -> p (s v)"),
+                    )
 
         def project(group, chunk):
             banks = [
@@ -164,7 +169,7 @@ def tile_transformer_block_pa_kernel(tc, x, w_qk_words, w_qk_scales, out):
                 nc.tensor.matmul_mx(
                     out=banks[h][lane // 2][:, lane % 2, :],
                     lhsT=x_codes[:, group, lane, positions].bitcast(FP8X4),
-                    lhsT_scale=x_scales[:, group, lane, positions],
+                    lhsT_scale=x_scales[:, group, lane, cpass, SCALE_BYTES],
                     rhs=w_codes[:, cpass, channels].bitcast(FP8X4),
                     rhs_scale=w_scales[4 * cpass : P, channels],
                     start=(cpass == 0),
@@ -191,12 +196,21 @@ def tile_transformer_block_pa_kernel(tc, x, w_qk_words, w_qk_scales, out):
             return grouped
 
         def quantise_qk(grouped, group, chunk):
-            channels = slice(chunk * CHUNK, (chunk + 1) * CHUNK)
-            nc.vector.quantize_mx(
-                out=qk_codes[:, group, channels].bitcast(FP8X4),
-                scales=qk_scales[:, group, channels],
-                in_=grouped[:].rearrange("p n u -> p (n u)").bitcast(BF16),
-            )
+            words = grouped[:].rearrange("p n u -> p (n u)").bitcast(BF16)
+            first = chunk * CHUNK
+            if first >= CH:
+                nc.vector.quantize_mx(
+                    out=qk_codes[:, group, first : first + CHUNK].bitcast(FP8X4),
+                    scales=k_scales[:, group, first - CH : first - CH + CHUNK],
+                    in_=words,
+                )
+            else:
+                for tile in range(CHUNK // P):
+                    nc.vector.quantize_mx(
+                        out=qk_codes[:, group, first + tile * P : first + (tile + 1) * P].bitcast(FP8X4),
+                        scales=q_scales[:, group, first // P + tile, SCALE_BYTES],
+                        in_=words[:, tile * P * PACK : (tile + 1) * P * PACK],
+                    )
 
         quantise_x(transpose_x(sort_x(0, range(1, PACK - 1)), zeros_between=1), 0)
         to_join = None
@@ -226,9 +240,9 @@ def tile_transformer_block_pa_kernel(tc, x, w_qk_words, w_qk_scales, out):
                 nc.tensor.matmul_mx(
                     out=sums[:],
                     lhsT=qk_codes[:, group, q_channels].bitcast(FP8X4),
-                    lhsT_scale=qk_scales[:, group, q_channels],
+                    lhsT_scale=q_scales[:, group, q_channels.start // P, SCALE_BYTES],
                     rhs=qk_codes[:, group, CH + first : CH + first + width].bitcast(FP8X4),
-                    rhs_scale=qk_scales[:, group, CH + first : CH + first + width],
+                    rhs_scale=k_scales[:, group, first : first + width],
                     start=(group == 0),
                     stop=(group == SEQ_GROUPS - 1),
                 )

import math
from contextlib import ExitStack

import concourse.mybir as mybir
from concourse.masks import make_identity

F32 = mybir.dt.float32
BF16 = mybir.dt.bfloat16
I32 = mybir.dt.int32
U32 = mybir.dt.uint32
U8 = mybir.dt.uint8
FP8X4 = mybir.dt.float8_e4m3fn_x4

P = 128
PACK = 4
K_PASS = P * PACK
BANK = 512
PSUM_BANKS = 8

SEQ = 1536
CH = 1024
QK = 2 * CH

CH_PASSES = CH // K_PASS
SEQ_GROUPS = SEQ // K_PASS
CHUNK = 512
HALF = CHUNK // 2
CHUNK_ORDER = (2, 0, 3, 1)

FIRST_COLUMNS = slice(CHUNK_ORDER[0] * CHUNK, CHUNK_ORDER[0] * CHUNK + CHUNK)
BEFORE_FIRST = slice(0, FIRST_COLUMNS.start)
BEHIND_FIRST = slice(FIRST_COLUMNS.stop, QK)

SCALE_STEP = 256
SCALE_BYTES = slice(SCALE_STEP // 2, SCALE_STEP)

WARM_UP_MATMULS = 4

FLOPS = 2 * QK * SEQ * CH + 2 * CH * CH * SEQ


def tile_transformer_block_pa_kernel(tc, x, w_qk_words, w_qk_scales, out):
    nc = tc.nc
    with ExitStack() as ctx:
        keep = ctx.enter_context(tc.tile_pool(name="keep", bufs=1))
        x_sort = ctx.enter_context(tc.tile_pool(name="x_sort", bufs=2))
        x_stage = ctx.enter_context(tc.tile_pool(name="x_stage", bufs=4))
        qk_pairs = ctx.enter_context(tc.tile_pool(name="qk_pairs", bufs=3))
        qk_stage = ctx.enter_context(tc.tile_pool(name="qk_stage", bufs=3))
        out_stage = ctx.enter_context(tc.tile_pool(name="out_stage", bufs=8))
        psum = ctx.enter_context(tc.psum_pool(name="psum", bufs=PSUM_BANKS))
        ctx.enter_context(tc.manual_schedule())

        identity = keep.tile([P, P], F32)
        x_rows = keep.tile([P, SEQ_GROUPS, PACK, CH], BF16)
        x_codes = keep.tile([P, SEQ_GROUPS, PACK, CH_PASSES * P], U32, align_bytes=64)
        x_scales = keep.tile([P, SEQ_GROUPS, PACK, CH_PASSES, SCALE_STEP], U8, align_bytes=SCALE_STEP)
        w_codes = keep.tile([P, CH_PASSES, QK], U32, align_bytes=64)
        w_scales = keep.tile([P, QK], U8, align_bytes=64)
        qk_codes = keep.tile([P, SEQ_GROUPS, QK], U32, align_bytes=64)
        q_scales = keep.tile([P, SEQ_GROUPS, CH // P, SCALE_STEP], U8, align_bytes=SCALE_STEP)
        k_scales = keep.tile([P, SEQ_GROUPS, CH], U8, align_bytes=SCALE_STEP)

        zeros = keep.tile([P, BANK], BF16)
        nc.vector.memset(w_scales[:, FIRST_COLUMNS].bitcast(I32), 0)
        nc.vector.memset(zeros[:].bitcast(F32), 0.0)
        unread = psum.tile([P, BANK], F32, tag="bank", name="unread")

        def multiply_zeros(times):
            for repeat in range(times):
                nc.tensor.matmul(unread[:], lhsT=zeros[:, 0:P], rhs=zeros[:], start=True, stop=True)

        multiply_zeros(WARM_UP_MATMULS)

        nc.vector.memset(w_scales[:, BEFORE_FIRST].bitcast(I32), 0)
        nc.vector.memset(w_scales[:, BEHIND_FIRST].bitcast(I32), 0)
        make_identity(nc, identity[:])

        x_by_group = x[0].rearrange("(group p lane) c -> group p (lane c)", p=P, lane=PACK)
        w_bytes = w_qk_words.rearrange("cpass p n v -> p cpass (n v)")

        def load_x(group, first_lane, lanes):
            columns = slice(first_lane * CH, (first_lane + lanes) * CH)
            nc.sync.dma_start(
                out=x_rows[:, group, :, :].rearrange("p lane c -> p (lane c)")[:, columns],
                in_=x_by_group[group, :, columns],
            )

        def load_w_scales(columns):
            for quarter in range(4):
                nc.sync.dma_start(
                    out=w_scales[32 * quarter : 32 * quarter + 4 * CH_PASSES, columns].bitcast(I32),
                    in_=w_qk_scales[:, 4 * quarter : 4 * quarter + 4, columns].bitcast(I32),
                )

        def load_w_codes(first, width):
            nc.sync.dma_start(
                out=w_codes[:, :, first : first + width].bitcast(I32),
                in_=w_bytes[:, :, first * PACK : (first + width) * PACK].bitcast(I32),
            )

        load_x(0, 0, 1)
        load_x(0, 1, 1)
        load_w_scales(FIRST_COLUMNS)
        load_x(0, 2, 1)
        load_x(0, 3, 1)
        load_w_codes(CHUNK_ORDER[0] * CHUNK, HALF)
        load_w_codes(CHUNK_ORDER[0] * CHUNK + HALF, HALF)
        load_w_codes(CHUNK_ORDER[1] * CHUNK, CHUNK)
        load_w_scales(BEFORE_FIRST)
        load_x(1, 0, 2)
        load_x(1, 2, 2)
        load_w_codes(CHUNK_ORDER[2] * CHUNK, CHUNK)
        load_w_scales(BEHIND_FIRST)
        load_w_codes(CHUNK_ORDER[3] * CHUNK, CHUNK)
        load_x(2, 0, PACK)

        def words_by_half(group, lane):
            words = x_rows[:, group, lane, :].bitcast(F32)
            return words.rearrange("p (cpass k half) -> p cpass half k", cpass=CH_PASSES, half=2)

        def sort_x(group, lanes):
            pairs = x_sort.tile([P, PACK, CH_PASSES, 2, P], F32)
            for lane in lanes:
                nc.vector.tensor_copy(out=pairs[:, lane, :, :, :], in_=words_by_half(group, lane))
            return [
                pairs[:, lane, :, :, :] if lane in lanes else words_by_half(group, lane) for lane in range(PACK)
            ]

        def transpose_x(pairs, zeros_between):
            grouped = []
            for lane in range(PACK):
                pairs_t = psum.tile([P, CH_PASSES, 2, P], F32, tag="bank")
                for cpass in range(CH_PASSES):
                    for half in range(2):
                        nc.tensor.transpose(
                            pairs_t[:, cpass, half, :], pairs[lane][:, cpass, half, :], identity[:]
                        )
                if lane < PACK - 1:
                    multiply_zeros(zeros_between)
                x_grouped = x_stage.tile([P, CH_PASSES, P, PACK], BF16, align_bytes=64)
                nc.scalar.copy(
                    out=x_grouped[:].bitcast(F32),
                    in_=pairs_t[:].rearrange("p cpass half s -> p cpass s half"),
                )
                grouped.append(x_grouped)
            return grouped

        def quantise_x(grouped, group):
            for lane in range(PACK):
                for cpass in range(CH_PASSES):
                    nc.vector.quantize_mx(
                        out=x_codes[:, group, lane, cpass * P : (cpass + 1) * P].bitcast(FP8X4),
                        scales=x_scales[:, group, lane, cpass, SCALE_BYTES],
                        in_=grouped[lane][:, cpass, :, :].rearrange("p s v -> p (s v)"),
                    )

        def project(group, chunk):
            banks = [
                [psum.tile([P, 2, HALF], F32, tag="bank", name="bank%d%d" % (h, u)) for u in range(2)]
                for h in range(2)
            ]
            order = [(h, lane) for h in range(2) for lane in range(PACK)]
            if (group, chunk) == (0, CHUNK_ORDER[0]):
                order = sorted(order, key=lambda h_lane: h_lane[1] + 1.5 * h_lane[0])
            for h, lane, cpass in [(h, lane, cpass) for h, lane in order for cpass in range(CH_PASSES)]:
                channels = slice(chunk * CHUNK + h * HALF, chunk * CHUNK + (h + 1) * HALF)
                positions = slice(cpass * P, (cpass + 1) * P)
                nc.tensor.matmul_mx(
                    out=banks[h][lane // 2][:, lane % 2, :],
                    lhsT=x_codes[:, group, lane, positions].bitcast(FP8X4),
                    lhsT_scale=x_scales[:, group, lane, cpass, SCALE_BYTES],
                    rhs=w_codes[:, cpass, channels].bitcast(FP8X4),
                    rhs_scale=w_scales[4 * cpass : P, channels],
                    start=(cpass == 0),
                    stop=(cpass == CH_PASSES - 1),
                )
            return banks

        def round_to_pairs(banks):
            pairs = qk_pairs.tile([P, 2, CHUNK], F32, align_bytes=64)
            for h in range(2):
                for u in range(2):
                    copy = nc.vector.tensor_copy if (h, u) == (0, 0) else nc.scalar.copy
                    copy(
                        out=pairs[:, u, h * HALF : (h + 1) * HALF]
                        .bitcast(BF16)
                        .rearrange("p (n lane) -> p n lane", lane=2),
                        in_=banks[h][u][:].rearrange("p lane n -> p n lane"),
                    )
            return pairs

        def join_pairs(pairs):
            grouped = qk_stage.tile([P, CHUNK, 2], F32, align_bytes=64)
            nc.vector.tensor_copy(out=grouped[:], in_=pairs[:].rearrange("p u n -> p n u"))
            return grouped

        def quantise_qk(grouped, group, chunk):
            words = grouped[:].rearrange("p n u -> p (n u)").bitcast(BF16)
            first = chunk * CHUNK
            if first >= CH:
                nc.vector.quantize_mx(
                    out=qk_codes[:, group, first : first + CHUNK].bitcast(FP8X4),
                    scales=k_scales[:, group, first - CH : first - CH + CHUNK],
                    in_=words,
                )
            else:
                for tile in range(CHUNK // P):
                    nc.vector.quantize_mx(
                        out=qk_codes[:, group, first + tile * P : first + (tile + 1) * P].bitcast(FP8X4),
                        scales=q_scales[:, group, first // P + tile, SCALE_BYTES],
                        in_=words[:, tile * P * PACK : (tile + 1) * P * PACK],
                    )

        quantise_x(transpose_x(sort_x(0, range(1, PACK - 1)), zeros_between=1), 0)
        to_join = None
        to_quantise = None
        for group in range(SEQ_GROUPS):
            for i, chunk in enumerate(CHUNK_ORDER):
                banks = project(group, chunk)
                if to_quantise is not None:
                    quantise_qk(*to_quantise)
                    to_quantise = None
                pairs = round_to_pairs(banks)
                if to_join is not None:
                    to_quantise = (join_pairs(to_join[0]), to_join[1], to_join[2])
                to_join = (pairs, group, chunk)
                if i == 0 and group + 1 < SEQ_GROUPS:
                    next_pairs = sort_x(group + 1, range(PACK))
                if i == 1 and group + 1 < SEQ_GROUPS:
                    next_x = transpose_x(next_pairs, zeros_between=0)
                if i == 2 and group + 1 < SEQ_GROUPS:
                    quantise_x(next_x, group + 1)
        quantise_qk(*to_quantise)
        quantise_qk(join_pairs(to_join[0]), to_join[1], to_join[2])

        def multiply_qk(q_channels, first, width, score, scale):
            sums = psum.tile([P, width], F32, tag="bank")
            for group in range(SEQ_GROUPS):
                nc.tensor.matmul_mx(
                    out=sums[:],
                    lhsT=qk_codes[:, group, q_channels].bitcast(FP8X4),
                    lhsT_scale=q_scales[:, group, q_channels.start // P, SCALE_BYTES],
                    rhs=qk_codes[:, group, CH + first : CH + first + width].bitcast(FP8X4),
                    rhs_scale=k_scales[:, group, first : first + width],
                    start=(group == 0),
                    stop=(group == SEQ_GROUPS - 1),
                )
            scale(score, sums[:])

        def scale_on_scalar(score, sums):
            nc.scalar.mul(out=score, in_=sums, mul=1.0 / math.sqrt(SEQ))

        def scale_on_vector(score, sums):
            nc.vector.tensor_scalar_mul(out=score, in0=sums, scalar1=1.0 / math.sqrt(SEQ))

        for q_first in range(0, CH, P):
            q_channels = slice(q_first, q_first + P)
            if q_first + P < CH:
                score = out_stage.tile([P, CH], F32)
                multiply_qk(q_channels, 0, BANK, score[:, 0:BANK], scale_on_scalar)
                multiply_qk(q_channels, BANK, BANK, score[:, BANK:CH], scale_on_vector)
                for columns in [slice(0, CH)] if q_first + 2 * P < CH else [slice(0, BANK), slice(BANK, CH)]:
                    nc.sync.dma_start(out=out[0, q_channels, columns], in_=score[:, columns])
            else:
                first = 0
                for width, scale in (
                    (BANK, scale_on_scalar),
                    (BANK // 2, scale_on_vector),
                    (BANK // 4, scale_on_scalar),
                    (BANK // 4, scale_on_vector),
                ):
                    piece = out_stage.tile([P, width], F32)
                    multiply_qk(q_channels, first, width, piece[:], scale)
                    nc.sync.dma_start(out=out[0, q_channels, first : first + width], in_=piece[:])
                    first += width
